import numpy as np
import ml_dtypes


BF16 = ml_dtypes.bfloat16


def bf(x):
    return np.asarray(x, np.float32).astype(BF16)


def f64(x):
    return np.asarray(x).astype(np.float64)


E2M1 = np.array([0.0, 0.5, 1.0, 1.5, 2.0, 3.0, 4.0, 6.0, -0.0, -0.5, -1.0, -1.5, -2.0, -3.0, -4.0, -6.0])


def pack_weight(w, fmt):
    k, n = w.shape
    w = f64(bf(w)).reshape(k // 32, 32, n)
    amax = np.abs(w).max(1)
    if fmt == "e4m3":
        byte = np.frexp(amax)[1] - 1 + 127 - 7
    else:
        mant, ex = np.frexp(amax / 6.0)
        byte = np.where(mant > 0.5, ex, ex - 1) + 127
    byte = np.clip(np.where(amax > 0, byte, 1), 1, 254)
    scaled = (w * np.exp2(127.0 - byte)[:, None, :]).reshape(k, n).astype(np.float32)
    by_word = np.ascontiguousarray(scaled.reshape(k // 512, 128, 4, n).transpose(0, 1, 3, 2))
    if fmt == "e4m3":
        words = by_word.astype(ml_dtypes.float8_e4m3fn).view(np.uint8)
    else:
        c = by_word.astype(ml_dtypes.float4_e2m1fn).view(np.uint8) & 0xF
        words = c[..., 0::2] | (c[..., 1::2] << 4)
    return np.ascontiguousarray(words), np.ascontiguousarray(byte.astype(np.uint8).reshape(k // 512, 16, n))


def unpack_weight(words, scales, fmt):
    g, p, n, _ = words.shape
    if fmt == "e4m3":
        vals = np.ascontiguousarray(words).view(ml_dtypes.float8_e4m3fn).astype(np.float64)
    else:
        nib = np.empty((g, p, n, 4), np.uint8)
        nib[..., 0::2] = words & 0xF
        nib[..., 1::2] = words >> 4
        vals = E2M1[nib]
    vals = vals * np.repeat(np.exp2(scales.astype(np.float64) - 127.0), 8, axis=1)[..., None]
    return vals.transpose(0, 1, 3, 2).reshape(g * 512, n)

def pack4(w):
    words, scales = pack_weight(w, "e2m1")
    return words.reshape(words.shape[0], 128, -1), scales


def unpack4(words, scales):
    return unpack_weight(words.reshape(words.shape[0], 128, -1, 2), scales, "e2m1")


def kspread(k):
    return np.exp2(np.repeat(np.random.randint(-6, 7, k // 32), 32).astype(np.float64))


B, S, H, NH, HD, TRAIN, NTK0, BASE = 1, 512, 1536, 16, 128, 8192, 4096, 10000


def rotary_cos_sin(seq_len):
    eff = max(seq_len, TRAIN)
    scale = eff / TRAIN
    mscale = 1.0 if scale <= 1.0 else 0.1 * np.log(scale) + 1.0
    p = 1
    while p < 2 * eff / NTK0:
        p *= 2
    ntk_alpha = max(p - 1, 1)
    base = BASE * ntk_alpha ** (HD / (HD - 2))
    inv_freq = 1.0 / base ** (np.arange(0, HD, 2, dtype=np.float64) / HD)
    freqs = np.outer(np.arange(eff, dtype=np.float64), inv_freq)
    emb = np.concatenate([freqs, freqs], axis=-1)
    return (mscale * np.cos(emb))[:seq_len], (mscale * np.sin(emb))[:seq_len]


def rotate_half(x):
    x1, x2 = x[..., : HD // 2], x[..., HD // 2 :]
    return np.concatenate([-x2, x1], axis=-1)


def setup_inputs():
    s = kspread(H)
    hidden_states = np.random.standard_normal((B, S, H)) * s
    wq = np.random.standard_normal((NH * HD, H)) / np.sqrt(H) / s
    wkv = np.random.standard_normal((2 * NH * HD, H)) / np.sqrt(H) / s
    hidden_states_words, hidden_states_scales = pack4(np.ascontiguousarray(hidden_states.reshape(B * S, H).T))
    Wq_words, Wq_scales = pack4(np.ascontiguousarray(wq.T))
    Wkv_words, Wkv_scales = pack4(np.ascontiguousarray(wkv.T))
    return {"hidden_states_words": hidden_states_words, "hidden_states_scales": hidden_states_scales,
            "Wq_words": Wq_words, "Wq_scales": Wq_scales,
            "Wkv_words": Wkv_words, "Wkv_scales": Wkv_scales}


def reference(hidden_states_words, hidden_states_scales, Wq_words, Wq_scales, Wkv_words, Wkv_scales):
    xq = unpack4(hidden_states_words, hidden_states_scales).T.reshape(B, S, H)
    q = (xq @ unpack4(Wq_words, Wq_scales)).reshape(B, S, NH, HD)
    kv = (xq @ unpack4(Wkv_words, Wkv_scales)).reshape(B, S, NH, 2 * HD)
    k, v = kv[..., :HD], kv[..., HD:]
    cos, sin = rotary_cos_sin(S)
    cos = cos[None, :, None, :]
    sin = sin[None, :, None, :]
    q_rot = q * cos + rotate_half(q) * sin
    k_rot = k * cos + rotate_half(k) * sin
    return q_rot, k_rot, v

@@ -1,0 +1,233 @@
+from contextlib import ExitStack
+import math
+
+import concourse.mybir as mybir
+
+F32 = mybir.dt.float32
+I32 = mybir.dt.int32
+U8 = mybir.dt.uint8
+FP4X4 = mybir.dt.float4_e2m1fn_x4
+ALU = mybir.AluOpType
+ACT = mybir.ActivationFunctionType
+
+P = 128
+S_LEN = 512
+K = 1536
+PASSES = K // 512
+NH = 16
+HD = 128
+HALF = HD // 2
+TT = S_LEN // P
+NT = 4
+FLOPS = 2 * S_LEN * K * (3 * NH * HD)
+
+ROPE_BASE = 10000.0 * 3.0 ** (128.0 / 126.0)
+RATIO = ROPE_BASE ** (-1.0 / 64.0)
+
+
+def tile_telechatattention_pa_kernel(tc, x_words, x_scales, wq_words, wq_scales, wkv_words, wkv_scales, out_q, out_k, out_v):
+    nc = tc.nc
+    with ExitStack() as ctx:
+        keep = ctx.enter_context(tc.tile_pool(name="keep", bufs=1))
+        work = ctx.enter_context(tc.tile_pool(name="work", bufs=8))
+        psum = ctx.enter_context(tc.psum_pool(name="psum", bufs=8))
+        ctx.enter_context(tc.manual_schedule())
+
+        xc = keep.tile([P, PASSES, 1024], U8, name="xc", align_bytes=64)
+        xs = keep.tile([P, PASSES, 512], U8, name="xs", align_bytes=64)
+        qc0 = keep.tile([P, PASSES, 1024], U8, name="qc0", align_bytes=64)
+        qs0 = keep.tile([P, PASSES, 512], U8, name="qs0", align_bytes=64)
+        qcr = keep.tile([P, PASSES, 3072], U8, name="qcr", align_bytes=64)
+        qsr = keep.tile([P, PASSES, 1536], U8, name="qsr", align_bytes=64)
+        kvc0 = keep.tile([P, PASSES, 2048], U8, name="kvc0", align_bytes=64)
+        kvs0 = keep.tile([P, PASSES, 1024], U8, name="kvs0", align_bytes=64)
+        kvc1 = keep.tile([P, PASSES, 2048], U8, name="kvc1", align_bytes=64)
+        kvcr = keep.tile([P, PASSES, 4096], U8, name="kvcr", align_bytes=64)
+        kvsr = keep.tile([P, PASSES, 3072], U8, name="kvsr", align_bytes=64)
+
+        def load_codes(dst, src, lo, hi):
+            nc.sync.dma_start(out=dst[:].bitcast(I32), in_=src[:, :, lo:hi].rearrange("g p n -> p g n").bitcast(I32))
+
+        def load_scales(dst, src, lo, hi):
+            for q in range(4):
+                nc.sync.dma_start(
+                    out=dst[32 * q : 32 * q + 4, :, :].bitcast(I32),
+                    in_=src[:, 4 * q : 4 * q + 4, lo:hi].rearrange("g r n -> r g n").bitcast(I32),
+                )
+
+        def zero(view):
+            nc.vector.memset(view.bitcast(I32), 0)
+
+        nc.gpsimd.memset(xs[:].bitcast(F32), 0.0)
+        pos = keep.tile([P, TT], F32, name="pos")
+        nc.gpsimd.iota(pos[:], pattern=[[P, TT]], base=0, channel_multiplier=1, allow_small_or_imprecise_dtypes=True)
+        load_codes(xc, x_words, 0, 1024)
+        load_scales(xs, x_scales, 0, 512)
+        load_codes(qc0, wq_words, 0, 1024)
+
+        fh = keep.tile([P, HALF], F32, name="fh")
+        nc.vector.memset(fh[:, 0:1], 0.5)
+
+        def spread(w):
+            for m in range(1, 4):
+                nc.vector.tensor_scalar(out=fh[:, m * w : (m + 1) * w], in0=fh[:, 0:w], scalar1=RATIO ** (m * w), scalar2=None, op0=ALU.mult)
+
+        spread(1)
+        zero(qs0[:])
+        load_scales(qs0, wq_scales, 0, 512)
+        load_codes(qcr, wq_words, 1024, 4096)
+        spread(4)
+        zero(qsr[:])
+        load_scales(qsr, wq_scales, 512, 2048)
+        load_codes(kvc0, wkv_words, 0, 2048)
+        spread(16)
+        hang = keep.tile([P, TT, HALF], F32, name="hang")
+        nc.vector.tensor_tensor(
+            out=hang[:],
+            in0=pos[:].unsqueeze(2).to_broadcast([P, TT, HALF]),
+            in1=fh[:].unsqueeze(1).to_broadcast([P, TT, HALF]),
+            op=ALU.mult,
+        )
+        flat = "p a j -> p (a j)"
+        turns = keep.tile([P, 2, TT, HALF], I32, name="turns")
+        red = keep.tile([P, 2, TT, HALF], F32, name="red")
+        sn = keep.tile([P, 2, TT, HALF], F32, name="sn")
+        sq = keep.tile([P, 2, TT, HALF], F32, name="sq")
+        for r in range(2):
+            nc.vector.tensor_scalar(out=turns[:, r, :, :].rearrange(flat), in0=hang[:].rearrange(flat), scalar1=1.0 / math.pi, scalar2=0.25 - 0.25 * r, op0=ALU.mult, op1=ALU.add)
+        for r in range(2):
+            nc.vector.scalar_tensor_tensor(out=red[:, r, :, :].rearrange(flat), in0=turns[:, r, :, :].rearrange(flat), scalar=-math.pi, in1=hang[:].rearrange(flat), op0=ALU.mult, op1=ALU.add)
+            nc.scalar.activation(out=sn[:, r, :, :].rearrange(flat), in_=red[:, r, :, :].rearrange(flat), func=ACT.Sin, bias=-0.25 * math.pi * r)
+        zero(kvs0[:])
+        load_scales(kvs0, wkv_scales, 0, 1024)
+        load_codes(kvc1, wkv_words, 2048, 4096)
+        load_codes(kvcr, wkv_words, 4096, 8192)
+        for r in range(2):
+            nc.vector.tensor_tensor(out=sq[:, r, :, :].rearrange(flat), in0=sn[:, r, :, :].rearrange(flat), in1=sn[:, r, :, :].rearrange(flat), op=ALU.mult)
+        tab = keep.tile([P, TT, 2, HD], F32, name="tab")
+        nc.vector.tensor_scalar(
+            out=tab[:, :, 0, :].rearrange("p a (h j) -> p a h j", h=2),
+            in0=sq[:, 0, :, :].unsqueeze(2).to_broadcast([P, TT, 2, HALF]),
+            scalar1=-2.0, scalar2=1.0, op0=ALU.mult, op1=ALU.add,
+        )
+        nc.vector.tensor_scalar(out=tab[:, :, 1, 0:HALF], in0=sq[:, 1, :, :], scalar1=-2.0, scalar2=1.0, op0=ALU.mult, op1=ALU.add)
+        nc.vector.tensor_scalar(out=tab[:, :, 1, HALF:HD], in0=sq[:, 1, :, :], scalar1=2.0, scalar2=-1.0, op0=ALU.mult, op1=ALU.add)
+
+        def project(codes, cblk, planes, pblk, a):
+            acc = psum.tile([P, 512], F32, name="acc")
+            for g in range(PASSES):
+                nc.tensor.matmul_mx(
+                    out=acc[:],
+                    lhsT=xc[:, g, 256 * a : 256 * (a + 1)].bitcast(FP4X4),
+                    lhsT_scale=xs[:, g, P * a : P * (a + 1)],
+                    rhs=codes[:, g, 1024 * cblk : 1024 * (cblk + 1)].bitcast(FP4X4),
+                    rhs_scale=planes[:, g, 512 * pblk : 512 * (pblk + 1)],
+                    start=(g == 0),
+                    stop=(g == PASSES - 1),
+                )
+            return acc
+
+        def mult(acc_view, heads, a, dst):
+            nc.vector.tensor_tensor(
+                out=dst.rearrange("p r (h d) -> p r h d", h=heads),
+                in0=acc_view.unsqueeze(1).to_broadcast([P, 2, heads, HD]),
+                in1=tab[:, a, :, :].unsqueeze(2).to_broadcast([P, 2, heads, HD]),
+                op=ALU.mult,
+            )
+
+        def q_bank(t, a, ut, col):
+            if t == 0:
+                acc = project(qc0, 0, qs0, 0, a)
+            else:
+                acc = project(qcr, t - 1, qsr, t - 1, a)
+            mult(acc[:].rearrange("p (h d) -> p h d", h=4), 4, a, ut[:, :, col : col + 512])
+
+        def kv_bank(t, a, blk, ut, col, ov, vector_first):
+            if t == 0:
+                acc = project(kvc0, blk, kvs0, blk, a)
+            elif t == 1:
+                acc = project(kvc1, blk, kvsr, blk, a)
+            else:
+                acc = project(kvcr, 2 * (t - 2) + blk, kvsr, 2 * (t - 1) + blk, a)
+            view = acc[:].rearrange("p (h w d) -> p h w d", h=2, w=2)
+            if vector_first:
+                mult(view[:, :, 0, :], 2, a, ut[:, :, col : col + 256])
+            nc.scalar.copy(out=ov[:, 256 * blk : 256 * (blk + 1)].rearrange("p (h d) -> p h d", h=2), in_=view[:, :, 1, :])
+            if not vector_first:
+                mult(view[:, :, 0, :], 2, a, ut[:, :, col : col + 256])
+
+        def store(dst, head, heads, a, src):
+            nc.sync.dma_start(out=dst[0, P * a : P * (a + 1), head : head + heads, :].rearrange("s h d -> s (h d)"), in_=src)
+
+        def rope_add(eng, ut, o):
+            split = "p (h w j) -> p h w j"
+            eng.tensor_tensor(
+                out=o[:].rearrange(split, w=2, j=HALF),
+                in0=ut[:, 0, :].rearrange(split, w=2, j=HALF),
+                in1=ut[:, 1, :].rearrange(split, w=2, j=HALF)[:, :, ::-1, :],
+                op=ALU.add,
+            )
+
+        held = []
+
+        def step(fresh):
+            for args in held:
+                store(*args)
+            held.clear()
+            held.extend(fresh)
+
+        def q_phase(t, span):
+            for a0 in range(0, TT, span):
+                ut = work.tile([P, 2, 512 * span], F32, name="ut")
+                for i in range(span):
+                    q_bank(t, a0 + i, ut, 512 * i)
+                o = work.tile([P, 512 * span], F32, name="o")
+                rope_add(nc.gpsimd, ut, o)
+                step([(out_q, 4 * t, 4, a0 + i, o[:, 512 * i : 512 * (i + 1)]) for i in range(span)])
+
+        def kv_phase(t, span):
+            for a0 in range(0, TT, span):
+                ut = work.tile([P, 2, 512 * span], F32, name="ut")
+                for i in range(span):
+                    ov = work.tile([P, 512], F32, name="ov")
+                    kv_bank(t, a0 + i, 0, ut, 512 * i, ov, False)
+                    kv_bank(t, a0 + i, 1, ut, 512 * i + 256, ov, False)
+                    store(out_v, 4 * t, 4, a0 + i, ov[:])
+                    if i + 1 < span:
+                        step([])
+                o = work.tile([P, 512 * span], F32, name="o")
+                rope_add(nc.gpsimd, ut, o)
+                step([(out_k, 4 * t, 4, a0 + i, o[:, 512 * i : 512 * (i + 1)]) for i in range(span)])
+
+        def last_kv_phase(t):
+            for a in range(TT - 1):
+                ut = work.tile([P, 2, 512], F32, name="ut")
+                ov = work.tile([P, 512], F32, name="ov")
+                kv_bank(t, a, 0, ut, 0, ov, False)
+                kv_bank(t, a, 1, ut, 256, ov, False)
+                store(out_v, 4 * t, 4, a, ov[:])
+                o = work.tile([P, 512], F32, name="o")
+                rope_add(nc.gpsimd, ut, o)
+                step([(out_k, 4 * t, 4, a, o[:])])
+            a = TT - 1
+            ut = work.tile([P, 2, 512], F32, name="ut")
+            ov = work.tile([P, 512], F32, name="ov")
+            kv_bank(t, a, 0, ut, 0, ov, False)
+            store(out_v, 4 * t, 2, a, ov[:, 0:256])
+            step([])
+            kv_bank(t, a, 1, ut, 256, ov, True)
+            o = work.tile([P, 512], F32, name="o")
+            rope_add(nc.vector, ut, o)
+            store(out_k, 4 * t, 4, a, o[:])
+            store(out_v, 4 * t + 2, 2, a, ov[:, 256:512])
+
+        q_phase(0, 1)
+        zero(kvsr[:])
+        load_scales(kvsr, wkv_scales, 1024, 4096)
+        q_phase(1, 2)
+        kv_phase(0, 2)
+        q_phase(2, 2)
+        kv_phase(1, 2)
+        q_phase(3, 2)
+        kv_phase(2, 2)
+        last_kv_phase(3)

@@ -43,7 +43,6 @@ def tile_telechatattention_pa_kernel(tc, x_words, x_scales, wq_words, wq_scales,
         kvs0 = keep.tile([P, PASSES, 1024], U8, name="kvs0", align_bytes=64)
         kvc1 = keep.tile([P, PASSES, 2048], U8, name="kvc1", align_bytes=64)
         kvcr = keep.tile([P, PASSES, 4096], U8, name="kvcr", align_bytes=64)
-        kvsr = keep.tile([P, PASSES, 3072], U8, name="kvsr", align_bytes=64)
 
         def load_codes(dst, src, lo, hi):
             nc.sync.dma_start(out=dst[:].bitcast(I32), in_=src[:, :, lo:hi].rearrange("g p n -> p g n").bitcast(I32))
@@ -146,9 +145,9 @@ def tile_telechatattention_pa_kernel(tc, x_words, x_scales, wq_words, wq_scales,
             if t == 0:
                 acc = project(kvc0, blk, kvs0, blk, a)
             elif t == 1:
-                acc = project(kvc1, blk, kvsr, blk, a)
+                acc = project(kvc1, blk, qc0, blk, a)
             else:
-                acc = project(kvcr, 2 * (t - 2) + blk, kvsr, 2 * (t - 1) + blk, a)
+                acc = project(kvcr, 2 * (t - 2) + blk, kvc0, 2 * (t - 2) + blk, a)
             view = acc[:].rearrange("p (h w d) -> p h w d", h=2, w=2)
             if vector_first:
                 mult(view[:, :, 0, :], 2, a, ut[:, :, col : col + 256])
@@ -222,10 +221,10 @@ def tile_telechatattention_pa_kernel(tc, x_words, x_scales, wq_words, wq_scales,
             store(out_v, 4 * t + 2, 2, a, ov[:, 256:512])
 
         q_phase(0, 1)
-        zero(kvsr[:])
-        load_scales(kvsr, wkv_scales, 1024, 4096)
+        load_scales(qc0, wkv_scales, 1024, 2048)
         q_phase(1, 2)
         kv_phase(0, 2)
+        load_scales(kvc0, wkv_scales, 2048, 4096)
         q_phase(2, 2)
         kv_phase(1, 2)
         q_phase(3, 2)

@@ -36,9 +36,9 @@ def tile_telechatattention_pa_kernel(tc, x_words, x_scales, wq_words, wq_scales,
         xc = keep.tile([P, PASSES, 1024], U8, name="xc", align_bytes=64)
         xs = keep.tile([P, PASSES, 512], U8, name="xs", align_bytes=64)
         qc0 = keep.tile([P, PASSES, 1024], U8, name="qc0", align_bytes=64)
-        qs0 = keep.tile([P, PASSES, 512], U8, name="qs0", align_bytes=64)
-        qcr = keep.tile([P, PASSES, 3072], U8, name="qcr", align_bytes=64)
-        qsr = keep.tile([P, PASSES, 1536], U8, name="qsr", align_bytes=64)
+        qc1 = keep.tile([P, PASSES, 1024], U8, name="qc1", align_bytes=64)
+        qs01 = keep.tile([P, PASSES, 1024], U8, name="qs01", align_bytes=64)
+        qc23 = keep.tile([P, PASSES, 2048], U8, name="qc23", align_bytes=64)
         kvc0 = keep.tile([P, PASSES, 2048], U8, name="kvc0", align_bytes=64)
         kvs0 = keep.tile([P, PASSES, 1024], U8, name="kvs0", align_bytes=64)
         kvc1 = keep.tile([P, PASSES, 2048], U8, name="kvc1", align_bytes=64)
@@ -72,13 +72,16 @@ def tile_telechatattention_pa_kernel(tc, x_words, x_scales, wq_words, wq_scales,
                 nc.vector.tensor_scalar(out=fh[:, m * w : (m + 1) * w], in0=fh[:, 0:w], scalar1=RATIO ** (m * w), scalar2=None, op0=ALU.mult)
 
         spread(1)
-        zero(qs0[:])
-        load_scales(qs0, wq_scales, 0, 512)
-        load_codes(qcr, wq_words, 1024, 4096)
+        zero(qs01[:])
+        load_scales(qs01, wq_scales, 0, 1024)
+        load_codes(qc1, wq_words, 1024, 2048)
         spread(4)
-        zero(qsr[:])
-        load_scales(qsr, wq_scales, 512, 2048)
+        zero(kvs0[:])
+        load_scales(kvs0, wkv_scales, 0, 1024)
         load_codes(kvc0, wkv_words, 0, 2048)
+        load_codes(qc23, wq_words, 2048, 4096)
+        load_codes(kvc1, wkv_words, 2048, 4096)
+        load_codes(kvcr, wkv_words, 4096, 8192)
         spread(16)
         hang = keep.tile([P, TT, HALF], F32, name="hang")
         nc.vector.tensor_tensor(
@@ -97,10 +100,6 @@ def tile_telechatattention_pa_kernel(tc, x_words, x_scales, wq_words, wq_scales,
         for r in range(2):
             nc.vector.scalar_tensor_tensor(out=red[:, r, :, :].rearrange(flat), in0=turns[:, r, :, :].rearrange(flat), scalar=-math.pi, in1=hang[:].rearrange(flat), op0=ALU.mult, op1=ALU.add)
             nc.scalar.activation(out=sn[:, r, :, :].rearrange(flat), in_=red[:, r, :, :].rearrange(flat), func=ACT.Sin, bias=-0.25 * math.pi * r)
-        zero(kvs0[:])
-        load_scales(kvs0, wkv_scales, 0, 1024)
-        load_codes(kvc1, wkv_words, 2048, 4096)
-        load_codes(kvcr, wkv_words, 4096, 8192)
         for r in range(2):
             nc.vector.tensor_tensor(out=sq[:, r, :, :].rearrange(flat), in0=sn[:, r, :, :].rearrange(flat), in1=sn[:, r, :, :].rearrange(flat), op=ALU.mult)
         tab = keep.tile([P, TT, 2, HD], F32, name="tab")
@@ -135,17 +134,17 @@ def tile_telechatattention_pa_kernel(tc, x_words, x_scales, wq_words, wq_scales,
             )
 
         def q_bank(t, a, ut, col):
-            if t == 0:
-                acc = project(qc0, 0, qs0, 0, a)
+            if t < 2:
+                acc = project(qc0 if t == 0 else qc1, 0, qs01, t, a)
             else:
-                acc = project(qcr, t - 1, qsr, t - 1, a)
+                acc = project(qc23, t - 2, qc0, t - 2, a)
             mult(acc[:].rearrange("p (h d) -> p h d", h=4), 4, a, ut[:, :, col : col + 512])
 
         def kv_bank(t, a, blk, ut, col, ov, vector_first):
             if t == 0:
                 acc = project(kvc0, blk, kvs0, blk, a)
             elif t == 1:
-                acc = project(kvc1, blk, qc0, blk, a)
+                acc = project(kvc1, blk, qc1, blk, a)
             else:
                 acc = project(kvcr, 2 * (t - 2) + blk, kvc0, 2 * (t - 2) + blk, a)
             view = acc[:].rearrange("p (h w d) -> p h w d", h=2, w=2)
@@ -221,8 +220,9 @@ def tile_telechatattention_pa_kernel(tc, x_words, x_scales, wq_words, wq_scales,
             store(out_v, 4 * t + 2, 2, a, ov[:, 256:512])
 
         q_phase(0, 1)
-        load_scales(qc0, wkv_scales, 1024, 2048)
+        load_scales(qc0, wq_scales, 1024, 2048)
         q_phase(1, 2)
+        load_scales(qc1, wkv_scales, 1024, 2048)
         kv_phase(0, 2)
         load_scales(kvc0, wkv_scales, 2048, 4096)
         q_phase(2, 2)

@@ -188,8 +188,8 @@ def tile_telechatattention_pa_kernel(tc, x_words, x_scales, wq_words, wq_scales,
                 ut = work.tile([P, 2, 512 * span], F32, name="ut")
                 for i in range(span):
                     ov = work.tile([P, 512], F32, name="ov")
-                    kv_bank(t, a0 + i, 0, ut, 512 * i, ov, False)
-                    kv_bank(t, a0 + i, 1, ut, 512 * i + 256, ov, False)
+                    kv_bank(t, a0 + i, 0, ut, 512 * i, ov, True)
+                    kv_bank(t, a0 + i, 1, ut, 512 * i + 256, ov, True)
                     store(out_v, 4 * t, 4, a0 + i, ov[:])
                     if i + 1 < span:
                         step([])
@@ -201,8 +201,8 @@ def tile_telechatattention_pa_kernel(tc, x_words, x_scales, wq_words, wq_scales,
             for a in range(TT - 1):
                 ut = work.tile([P, 2, 512], F32, name="ut")
                 ov = work.tile([P, 512], F32, name="ov")
-                kv_bank(t, a, 0, ut, 0, ov, False)
-                kv_bank(t, a, 1, ut, 256, ov, False)
+                kv_bank(t, a, 0, ut, 0, ov, True)
+                kv_bank(t, a, 1, ut, 256, ov, True)
                 store(out_v, 4 * t, 4, a, ov[:])
                 o = work.tile([P, 512], F32, name="o")
                 rope_add(nc.gpsimd, ut, o)
@@ -210,7 +210,7 @@ def tile_telechatattention_pa_kernel(tc, x_words, x_scales, wq_words, wq_scales,
             a = TT - 1
             ut = work.tile([P, 2, 512], F32, name="ut")
             ov = work.tile([P, 512], F32, name="ov")
-            kv_bank(t, a, 0, ut, 0, ov, False)
+            kv_bank(t, a, 0, ut, 0, ov, True)
             store(out_v, 4 * t, 2, a, ov[:, 0:256])
             step([])
             kv_bank(t, a, 1, ut, 256, ov, True)

@@ -48,10 +48,10 @@ def tile_telechatattention_pa_kernel(tc, x_words, x_scales, wq_words, wq_scales,
             nc.sync.dma_start(out=dst[:].bitcast(I32), in_=src[:, :, lo:hi].rearrange("g p n -> p g n").bitcast(I32))
 
         def load_scales(dst, src, lo, hi):
-            for q in range(4):
+            for r in range(4):
                 nc.sync.dma_start(
-                    out=dst[32 * q : 32 * q + 4, :, :].bitcast(I32),
-                    in_=src[:, 4 * q : 4 * q + 4, lo:hi].rearrange("g r n -> r g n").bitcast(I32),
+                    out=dst[r : P : 32, :, :].bitcast(I32),
+                    in_=src[:, r : 16 : 4, lo:hi].rearrange("g q n -> q g n").bitcast(I32),
                 )
 
         def zero(view):

@@ -4,6 +4,7 @@ import math
 import concourse.mybir as mybir
 
 F32 = mybir.dt.float32
+BF16 = mybir.dt.bfloat16
 I32 = mybir.dt.int32
 U8 = mybir.dt.uint8
 FP4X4 = mybir.dt.float4_e2m1fn_x4
@@ -19,6 +20,7 @@ HD = 128
 HALF = HD // 2
 TT = S_LEN // P
 NT = 4
+WARM = 12
 FLOPS = 2 * S_LEN * K * (3 * NH * HD)
 
 ROPE_BASE = 10000.0 * 3.0 ** (128.0 / 126.0)
@@ -58,6 +60,11 @@ def tile_telechatattention_pa_kernel(tc, x_words, x_scales, wq_words, wq_scales,
             nc.vector.memset(view.bitcast(I32), 0)
 
         nc.gpsimd.memset(xs[:].bitcast(F32), 0.0)
+        idle = keep.tile([P, 512], BF16, name="idle")
+        nc.gpsimd.memset(idle[:].bitcast(F32), 0.0)
+        warm = psum.tile([P, 512], F32, name="acc")
+        for i in range(WARM):
+            nc.tensor.matmul(out=warm[:], lhsT=idle[:, 0:P], rhs=idle[:], start=True, stop=True)
         pos = keep.tile([P, TT], F32, name="pos")
         nc.gpsimd.iota(pos[:], pattern=[[P, TT]], base=0, channel_multiplier=1, allow_small_or_imprecise_dtypes=True)
         load_codes(xc, x_words, 0, 1024)

@@ -35,16 +35,16 @@ def tile_telechatattention_pa_kernel(tc, x_words, x_scales, wq_words, wq_scales,
         psum = ctx.enter_context(tc.psum_pool(name="psum", bufs=8))
         ctx.enter_context(tc.manual_schedule())
 
-        xc = keep.tile([P, PASSES, 1024], U8, name="xc", align_bytes=64)
-        xs = keep.tile([P, PASSES, 512], U8, name="xs", align_bytes=64)
-        qc0 = keep.tile([P, PASSES, 1024], U8, name="qc0", align_bytes=64)
-        qc1 = keep.tile([P, PASSES, 1024], U8, name="qc1", align_bytes=64)
-        qs01 = keep.tile([P, PASSES, 1024], U8, name="qs01", align_bytes=64)
-        qc23 = keep.tile([P, PASSES, 2048], U8, name="qc23", align_bytes=64)
-        kvc0 = keep.tile([P, PASSES, 2048], U8, name="kvc0", align_bytes=64)
-        kvs0 = keep.tile([P, PASSES, 1024], U8, name="kvs0", align_bytes=64)
-        kvc1 = keep.tile([P, PASSES, 2048], U8, name="kvc1", align_bytes=64)
-        kvcr = keep.tile([P, PASSES, 4096], U8, name="kvcr", align_bytes=64)
+        xc = keep.tile([P, PASSES, 1024], U8, name="xc", align_bytes=256)
+        xs = keep.tile([P, PASSES, 512], U8, name="xs", align_bytes=256)
+        qc0 = keep.tile([P, PASSES, 1024], U8, name="qc0", align_bytes=256)
+        qc1 = keep.tile([P, PASSES, 1024], U8, name="qc1", align_bytes=256)
+        qs01 = keep.tile([P, PASSES, 1024], U8, name="qs01", align_bytes=256)
+        qc23 = keep.tile([P, PASSES, 2048], U8, name="qc23", align_bytes=256)
+        kvc0 = keep.tile([P, PASSES, 2048], U8, name="kvc0", align_bytes=256)
+        kvs0 = keep.tile([P, PASSES, 1024], U8, name="kvs0", align_bytes=256)
+        kvc1 = keep.tile([P, PASSES, 2048], U8, name="kvc1", align_bytes=256)
+        kvcr = keep.tile([P, PASSES, 4096], U8, name="kvcr", align_bytes=256)
 
         def load_codes(dst, src, lo, hi):
             nc.sync.dma_start(out=dst[:].bitcast(I32), in_=src[:, :, lo:hi].rearrange("g p n -> p g n").bitcast(I32))
@@ -183,45 +183,45 @@ def tile_telechatattention_pa_kernel(tc, x_words, x_scales, wq_words, wq_scales,
 
         def q_phase(t, span):
             for a0 in range(0, TT, span):
-                ut = work.tile([P, 2, 512 * span], F32, name="ut")
+                ut = work.tile([P, 2, 512 * span], F32, name="ut", align_bytes=256)
                 for i in range(span):
                     q_bank(t, a0 + i, ut, 512 * i)
-                o = work.tile([P, 512 * span], F32, name="o")
+                o = work.tile([P, 512 * span], F32, name="o", align_bytes=256)
                 rope_add(nc.gpsimd, ut, o)
                 step([(out_q, 4 * t, 4, a0 + i, o[:, 512 * i : 512 * (i + 1)]) for i in range(span)])
 
         def kv_phase(t, span):
             for a0 in range(0, TT, span):
-                ut = work.tile([P, 2, 512 * span], F32, name="ut")
+                ut = work.tile([P, 2, 512 * span], F32, name="ut", align_bytes=256)
                 for i in range(span):
-                    ov = work.tile([P, 512], F32, name="ov")
+                    ov = work.tile([P, 512], F32, name="ov", align_bytes=256)
                     kv_bank(t, a0 + i, 0, ut, 512 * i, ov, True)
                     kv_bank(t, a0 + i, 1, ut, 512 * i + 256, ov, True)
                     store(out_v, 4 * t, 4, a0 + i, ov[:])
                     if i + 1 < span:
                         step([])
-                o = work.tile([P, 512 * span], F32, name="o")
+                o = work.tile([P, 512 * span], F32, name="o", align_bytes=256)
                 rope_add(nc.gpsimd, ut, o)
                 step([(out_k, 4 * t, 4, a0 + i, o[:, 512 * i : 512 * (i + 1)]) for i in range(span)])
 
         def last_kv_phase(t):
             for a in range(TT - 1):
-                ut = work.tile([P, 2, 512], F32, name="ut")
-                ov = work.tile([P, 512], F32, name="ov")
+                ut = work.tile([P, 2, 512], F32, name="ut", align_bytes=256)
+                ov = work.tile([P, 512], F32, name="ov", align_bytes=256)
                 kv_bank(t, a, 0, ut, 0, ov, True)
                 kv_bank(t, a, 1, ut, 256, ov, True)
                 store(out_v, 4 * t, 4, a, ov[:])
-                o = work.tile([P, 512], F32, name="o")
+                o = work.tile([P, 512], F32, name="o", align_bytes=256)
                 rope_add(nc.gpsimd, ut, o)
                 step([(out_k, 4 * t, 4, a, o[:])])
             a = TT - 1
-            ut = work.tile([P, 2, 512], F32, name="ut")
-            ov = work.tile([P, 512], F32, name="ov")
+            ut = work.tile([P, 2, 512], F32, name="ut", align_bytes=256)
+            ov = work.tile([P, 512], F32, name="ov", align_bytes=256)
             kv_bank(t, a, 0, ut, 0, ov, True)
             store(out_v, 4 * t, 2, a, ov[:, 0:256])
             step([])
             kv_bank(t, a, 1, ut, 256, ov, True)
-            o = work.tile([P, 512], F32, name="o")
+            o = work.tile([P, 512], F32, name="o", align_bytes=256)
             rope_add(nc.vector, ut, o)
             store(out_k, 4 * t, 4, a, o[:])
             store(out_v, 4 * t + 2, 2, a, ov[:, 256:512])

@@ -88,7 +88,6 @@ def tile_telechatattention_pa_kernel(tc, x_words, x_scales, wq_words, wq_scales,
         load_codes(kvc0, wkv_words, 0, 2048)
         load_codes(qc23, wq_words, 2048, 4096)
         load_codes(kvc1, wkv_words, 2048, 4096)
-        load_codes(kvcr, wkv_words, 4096, 8192)
         spread(16)
         hang = keep.tile([P, TT, HALF], F32, name="hang")
         nc.vector.tensor_tensor(
@@ -175,28 +174,33 @@ def tile_telechatattention_pa_kernel(tc, x_words, x_scales, wq_words, wq_scales,
 
         held = []
 
-        def step(fresh):
-            for args in held:
-                store(*args)
-            held.clear()
-            held.extend(fresh)
+        def step(fresh, hold=2):
+            held.append(fresh)
+            for k in range(len(held) - hold):
+                for args in held[0]:
+                    store(*args)
+                held.remove(held[0])
 
-        def q_phase(t, span):
+        def q_phase(t, span, freed=None):
             for a0 in range(0, TT, span):
                 ut = work.tile([P, 2, 512 * span], F32, name="ut", align_bytes=256)
                 for i in range(span):
                     q_bank(t, a0 + i, ut, 512 * i)
+                if freed is not None and a0 + span == TT:
+                    freed()
                 o = work.tile([P, 512 * span], F32, name="o", align_bytes=256)
                 rope_add(nc.gpsimd, ut, o)
                 step([(out_q, 4 * t, 4, a0 + i, o[:, 512 * i : 512 * (i + 1)]) for i in range(span)])
 
-        def kv_phase(t, span):
+        def kv_phase(t, span, freed=None):
             for a0 in range(0, TT, span):
                 ut = work.tile([P, 2, 512 * span], F32, name="ut", align_bytes=256)
                 for i in range(span):
                     ov = work.tile([P, 512], F32, name="ov", align_bytes=256)
                     kv_bank(t, a0 + i, 0, ut, 512 * i, ov, True)
                     kv_bank(t, a0 + i, 1, ut, 512 * i + 256, ov, True)
+                    if freed is not None and a0 + i + 1 == TT:
+                        freed()
                     store(out_v, 4 * t, 4, a0 + i, ov[:])
                     if i + 1 < span:
                         step([])
@@ -213,25 +217,26 @@ def tile_telechatattention_pa_kernel(tc, x_words, x_scales, wq_words, wq_scales,
                 store(out_v, 4 * t, 4, a, ov[:])
                 o = work.tile([P, 512], F32, name="o", align_bytes=256)
                 rope_add(nc.gpsimd, ut, o)
-                step([(out_k, 4 * t, 4, a, o[:])])
+                step([(out_k, 4 * t, 4, a, o[:])], 1)
             a = TT - 1
             ut = work.tile([P, 2, 512], F32, name="ut", align_bytes=256)
             ov = work.tile([P, 512], F32, name="ov", align_bytes=256)
             kv_bank(t, a, 0, ut, 0, ov, True)
             store(out_v, 4 * t, 2, a, ov[:, 0:256])
-            step([])
+            step([], 0)
             kv_bank(t, a, 1, ut, 256, ov, True)
             o = work.tile([P, 512], F32, name="o", align_bytes=256)
             rope_add(nc.vector, ut, o)
             store(out_k, 4 * t, 4, a, o[:])
             store(out_v, 4 * t + 2, 2, a, ov[:, 256:512])
 
-        q_phase(0, 1)
-        load_scales(qc0, wq_scales, 1024, 2048)
-        q_phase(1, 2)
-        load_scales(qc1, wkv_scales, 1024, 2048)
-        kv_phase(0, 2)
-        load_scales(kvc0, wkv_scales, 2048, 4096)
+        def after_q1():
+            load_scales(qc1, wkv_scales, 1024, 2048)
+            load_codes(kvcr, wkv_words, 4096, 8192)
+
+        q_phase(0, 1, lambda: load_scales(qc0, wq_scales, 1024, 2048))
+        q_phase(1, 2, after_q1)
+        kv_phase(0, 2, lambda: load_scales(kvc0, wkv_scales, 2048, 4096))
         q_phase(2, 2)
         kv_phase(1, 2)
         q_phase(3, 2)

@@ -181,8 +181,34 @@ def tile_telechatattention_pa_kernel(tc, x_words, x_scales, wq_words, wq_scales,
                     store(*args)
                 held.remove(held[0])
 
-        def q_phase(t, span, freed=None):
-            for a0 in range(0, TT, span):
+        def first_unit():
+            ut = work.tile([P, 2, 512], F32, name="ut", align_bytes=256)
+            o = work.tile([P, 512], F32, name="o", align_bytes=256)
+            split = "p (h w j) -> p h w j"
+            for half in range(2):
+                acc = psum.tile([P, 512], F32, name="acc")
+                for g in range(PASSES):
+                    nc.tensor.matmul_mx(
+                        out=acc[:, 0:256],
+                        lhsT=xc[:, g, 0:256].bitcast(FP4X4),
+                        lhsT_scale=xs[:, g, 0:P],
+                        rhs=qc0[:, g, 512 * half : 512 * (half + 1)].bitcast(FP4X4),
+                        rhs_scale=qs01[:, g, 256 * half : 256 * (half + 1)],
+                        start=(g == 0),
+                        stop=(g == PASSES - 1),
+                    )
+                cols = slice(256 * half, 256 * (half + 1))
+                mult(acc[:, 0:256].rearrange("p (h d) -> p h d", h=2), 2, 0, ut[:, :, cols])
+                nc.gpsimd.tensor_tensor(
+                    out=o[:, cols].rearrange(split, w=2, j=HALF),
+                    in0=ut[:, 0, cols].rearrange(split, w=2, j=HALF),
+                    in1=ut[:, 1, cols].rearrange(split, w=2, j=HALF)[:, :, ::-1, :],
+                    op=ALU.add,
+                )
+            step([(out_q, 0, 4, 0, o[:])])
+
+        def q_phase(t, span, freed=None, first=0):
+            for a0 in range(first, TT, span):
                 ut = work.tile([P, 2, 512 * span], F32, name="ut", align_bytes=256)
                 for i in range(span):
                     q_bank(t, a0 + i, ut, 512 * i)
@@ -234,7 +260,8 @@ def tile_telechatattention_pa_kernel(tc, x_words, x_scales, wq_words, wq_scales,
             load_scales(qc1, wkv_scales, 1024, 2048)
             load_codes(kvcr, wkv_words, 4096, 8192)
 
-        q_phase(0, 1, lambda: load_scales(qc0, wq_scales, 1024, 2048))
+        first_unit()
+        q_phase(0, 1, lambda: load_scales(qc0, wq_scales, 1024, 2048), 1)
         q_phase(1, 2, after_q1)
         kv_phase(0, 2, lambda: load_scales(kvc0, wkv_scales, 2048, 4096))
         q_phase(2, 2)

@@ -108,7 +108,7 @@ def tile_telechatattention_pa_kernel(tc, x_words, x_scales, wq_words, wq_scales,
             nc.scalar.activation(out=sn[:, r, :, :].rearrange(flat), in_=red[:, r, :, :].rearrange(flat), func=ACT.Sin, bias=-0.25 * math.pi * r)
         for r in range(2):
             nc.vector.tensor_tensor(out=sq[:, r, :, :].rearrange(flat), in0=sn[:, r, :, :].rearrange(flat), in1=sn[:, r, :, :].rearrange(flat), op=ALU.mult)
-        tab = keep.tile([P, TT, 2, HD], F32, name="tab")
+        tab = keep.tile([P, TT, 2, HD], F32, name="tab", align_bytes=256)
         nc.vector.tensor_scalar(
             out=tab[:, :, 0, :].rearrange("p a (h j) -> p a h j", h=2),
             in0=sq[:, 0, :, :].unsqueeze(2).to_broadcast([P, TT, 2, HALF]),
@@ -163,12 +163,12 @@ def tile_telechatattention_pa_kernel(tc, x_words, x_scales, wq_words, wq_scales,
         def store(dst, head, heads, a, src):
             nc.sync.dma_start(out=dst[0, P * a : P * (a + 1), head : head + heads, :].rearrange("s h d -> s (h d)"), in_=src)
 
-        def rope_add(eng, ut, o):
+        def rope_add(eng, ut, o, cols=slice(None)):
             split = "p (h w j) -> p h w j"
             eng.tensor_tensor(
-                out=o[:].rearrange(split, w=2, j=HALF),
-                in0=ut[:, 0, :].rearrange(split, w=2, j=HALF),
-                in1=ut[:, 1, :].rearrange(split, w=2, j=HALF)[:, :, ::-1, :],
+                out=o[:, cols].rearrange(split, w=2, j=HALF),
+                in0=ut[:, 0, cols].rearrange(split, w=2, j=HALF),
+                in1=ut[:, 1, cols].rearrange(split, w=2, j=HALF)[:, :, ::-1, :],
                 op=ALU.add,
             )
 
@@ -247,14 +247,31 @@ def tile_telechatattention_pa_kernel(tc, x_words, x_scales, wq_words, wq_scales,
             a = TT - 1
             ut = work.tile([P, 2, 512], F32, name="ut", align_bytes=256)
             ov = work.tile([P, 512], F32, name="ov", align_bytes=256)
-            kv_bank(t, a, 0, ut, 0, ov, True)
-            store(out_v, 4 * t, 2, a, ov[:, 0:256])
-            step([], 0)
-            kv_bank(t, a, 1, ut, 256, ov, True)
             o = work.tile([P, 512], F32, name="o", align_bytes=256)
+            for w in range(2):
+                for pair in range(2):
+                    blk = 2 * (t - 2) + pair
+                    acc = psum.tile([P, 512], F32, name="acc")
+                    for h in range(2):
+                        for g in range(PASSES):
+                            nc.tensor.matmul_mx(
+                                out=acc[:, HD * h : HD * (h + 1)],
+                                lhsT=xc[:, g, 256 * a : 256 * (a + 1)].bitcast(FP4X4),
+                                lhsT_scale=xs[:, g, P * a : P * (a + 1)],
+                                rhs=kvcr[:, g, 1024 * blk + 512 * h + 256 * w : 1024 * blk + 512 * h + 256 * (w + 1)].bitcast(FP4X4),
+                                rhs_scale=kvc0[:, g, 512 * blk + 256 * h + HD * w : 512 * blk + 256 * h + HD * (w + 1)],
+                                start=(g == 0),
+                                stop=(g == PASSES - 1),
+                            )
+                    cols = slice(256 * pair, 256 * (pair + 1))
+                    if w == 0:
+                        mult(acc[:, 0:256].rearrange("p (h d) -> p h d", h=2), 2, a, ut[:, :, cols])
+                    else:
+                        nc.scalar.copy(out=ov[:, cols], in_=acc[:, 0:256])
             rope_add(nc.vector, ut, o)
+            store(out_v, 4 * t, 4, a, ov[:])
+            step([], 0)
             store(out_k, 4 * t, 4, a, o[:])
-            store(out_v, 4 * t + 2, 2, a, ov[:, 256:512])
 
         def after_q1():
             load_scales(qc1, wkv_scales, 1024, 2048)

@@ -182,7 +182,7 @@ def tile_telechatattention_pa_kernel(tc, x_words, x_scales, wq_words, wq_scales,
                 held.remove(held[0])
 
         def first_unit():
-            ut = work.tile([P, 2, 512], F32, name="ut", align_bytes=256)
+            ut = work.tile([P, 2, 512], F32, name="ut")
             o = work.tile([P, 512], F32, name="o", align_bytes=256)
             split = "p (h w j) -> p h w j"
             for half in range(2):
@@ -209,7 +209,7 @@ def tile_telechatattention_pa_kernel(tc, x_words, x_scales, wq_words, wq_scales,
 
         def q_phase(t, span, freed=None, first=0):
             for a0 in range(first, TT, span):
-                ut = work.tile([P, 2, 512 * span], F32, name="ut", align_bytes=256)
+                ut = work.tile([P, 2, 512 * span], F32, name="ut")
                 for i in range(span):
                     q_bank(t, a0 + i, ut, 512 * i)
                 if freed is not None and a0 + span == TT:
@@ -220,7 +220,7 @@ def tile_telechatattention_pa_kernel(tc, x_words, x_scales, wq_words, wq_scales,
 
         def kv_phase(t, span, freed=None):
             for a0 in range(0, TT, span):
-                ut = work.tile([P, 2, 512 * span], F32, name="ut", align_bytes=256)
+                ut = work.tile([P, 2, 512 * span], F32, name="ut")
                 for i in range(span):
                     ov = work.tile([P, 512], F32, name="ov", align_bytes=256)
                     kv_bank(t, a0 + i, 0, ut, 512 * i, ov, True)
@@ -236,7 +236,7 @@ def tile_telechatattention_pa_kernel(tc, x_words, x_scales, wq_words, wq_scales,
 
         def last_kv_phase(t):
             for a in range(TT - 1):
-                ut = work.tile([P, 2, 512], F32, name="ut", align_bytes=256)
+                ut = work.tile([P, 2, 512], F32, name="ut")
                 ov = work.tile([P, 512], F32, name="ov", align_bytes=256)
                 kv_bank(t, a, 0, ut, 0, ov, True)
                 kv_bank(t, a, 1, ut, 256, ov, True)
@@ -245,7 +245,7 @@ def tile_telechatattention_pa_kernel(tc, x_words, x_scales, wq_words, wq_scales,
                 rope_add(nc.gpsimd, ut, o)
                 step([(out_k, 4 * t, 4, a, o[:])], 1)
             a = TT - 1
-            ut = work.tile([P, 2, 512], F32, name="ut", align_bytes=256)
+            ut = work.tile([P, 2, 512], F32, name="ut")
             ov = work.tile([P, 512], F32, name="ov", align_bytes=256)
             o = work.tile([P, 512], F32, name="o", align_bytes=256)
             for w in range(2):
@@ -282,7 +282,7 @@ def tile_telechatattention_pa_kernel(tc, x_words, x_scales, wq_words, wq_scales,
         q_phase(1, 2, after_q1)
         kv_phase(0, 2, lambda: load_scales(kvc0, wkv_scales, 2048, 4096))
         q_phase(2, 2)
-        kv_phase(1, 2)
         q_phase(3, 2)
+        kv_phase(1, 2)
         kv_phase(2, 2)
         last_kv_phase(3)

from contextlib import ExitStack
import math

import concourse.mybir as mybir

F32 = mybir.dt.float32
BF16 = mybir.dt.bfloat16
I32 = mybir.dt.int32
U8 = mybir.dt.uint8
FP4X4 = mybir.dt.float4_e2m1fn_x4
ALU = mybir.AluOpType
ACT = mybir.ActivationFunctionType

P = 128
S_LEN = 512
K = 1536
PASSES = K // 512
NH = 16
HD = 128
HALF = HD // 2
TT = S_LEN // P
NT = 4
WARM = 12
FLOPS = 2 * S_LEN * K * (3 * NH * HD)

ROPE_BASE = 10000.0 * 3.0 ** (128.0 / 126.0)
RATIO = ROPE_BASE ** (-1.0 / 64.0)


def tile_telechatattention_pa_kernel(tc, x_words, x_scales, wq_words, wq_scales, wkv_words, wkv_scales, out_q, out_k, out_v):
    nc = tc.nc
    with ExitStack() as ctx:
        keep = ctx.enter_context(tc.tile_pool(name="keep", bufs=1))
        work = ctx.enter_context(tc.tile_pool(name="work", bufs=8))
        psum = ctx.enter_context(tc.psum_pool(name="psum", bufs=8))
        ctx.enter_context(tc.manual_schedule())

        xc = keep.tile([P, PASSES, 1024], U8, name="xc", align_bytes=256)
        xs = keep.tile([P, PASSES, 512], U8, name="xs", align_bytes=256)
        qc0 = keep.tile([P, PASSES, 1024], U8, name="qc0", align_bytes=256)
        qc1 = keep.tile([P, PASSES, 1024], U8, name="qc1", align_bytes=256)
        qs01 = keep.tile([P, PASSES, 1024], U8, name="qs01", align_bytes=256)
        qc23 = keep.tile([P, PASSES, 2048], U8, name="qc23", align_bytes=256)
        kvc0 = keep.tile([P, PASSES, 2048], U8, name="kvc0", align_bytes=256)
        kvs0 = keep.tile([P, PASSES, 1024], U8, name="kvs0", align_bytes=256)
        kvc1 = keep.tile([P, PASSES, 2048], U8, name="kvc1", align_bytes=256)
        kvcr = keep.tile([P, PASSES, 4096], U8, name="kvcr", align_bytes=256)

        def load_codes(dst, src, lo, hi):
            nc.sync.dma_start(out=dst[:].bitcast(I32), in_=src[:, :, lo:hi].rearrange("g p n -> p g n").bitcast(I32))

        def load_scales(dst, src, lo, hi):
            for r in range(4):
                nc.sync.dma_start(
                    out=dst[r : P : 32, :, :].bitcast(I32),
                    in_=src[:, r : 16 : 4, lo:hi].rearrange("g q n -> q g n").bitcast(I32),
                )

        def zero(view):
            nc.vector.memset(view.bitcast(I32), 0)

        nc.gpsimd.memset(xs[:].bitcast(F32), 0.0)
        idle = keep.tile([P, 512], BF16, name="idle")
        nc.gpsimd.memset(idle[:].bitcast(F32), 0.0)
        warm = psum.tile([P, 512], F32, name="acc")
        for i in range(WARM):
            nc.tensor.matmul(out=warm[:], lhsT=idle[:, 0:P], rhs=idle[:], start=True, stop=True)
        pos = keep.tile([P, TT], F32, name="pos")
        nc.gpsimd.iota(pos[:], pattern=[[P, TT]], base=0, channel_multiplier=1, allow_small_or_imprecise_dtypes=True)
        load_codes(xc, x_words, 0, 1024)
        load_scales(xs, x_scales, 0, 512)
        load_codes(qc0, wq_words, 0, 1024)

        fh = keep.tile([P, HALF], F32, name="fh")
        nc.vector.memset(fh[:, 0:1], 0.5)

        def spread(w):
            for m in range(1, 4):
                nc.vector.tensor_scalar(out=fh[:, m * w : (m + 1) * w], in0=fh[:, 0:w], scalar1=RATIO ** (m * w), scalar2=None, op0=ALU.mult)

        spread(1)
        zero(qs01[:])
        load_scales(qs01, wq_scales, 0, 1024)
        load_codes(qc1, wq_words, 1024, 2048)
        spread(4)
        zero(kvs0[:])
        load_scales(kvs0, wkv_scales, 0, 1024)
        load_codes(kvc0, wkv_words, 0, 2048)
        load_codes(qc23, wq_words, 2048, 4096)
        load_codes(kvc1, wkv_words, 2048, 4096)
        spread(16)
        hang = keep.tile([P, TT, HALF], F32, name="hang")
        nc.vector.tensor_tensor(
            out=hang[:],
            in0=pos[:].unsqueeze(2).to_broadcast([P, TT, HALF]),
            in1=fh[:].unsqueeze(1).to_broadcast([P, TT, HALF]),
            op=ALU.mult,
        )
        flat = "p a j -> p (a j)"
        turns = keep.tile([P, 2, TT, HALF], I32, name="turns")
        red = keep.tile([P, 2, TT, HALF], F32, name="red")
        sn = keep.tile([P, 2, TT, HALF], F32, name="sn")
        sq = keep.tile([P, 2, TT, HALF], F32, name="sq")
        for r in range(2):
            nc.vector.tensor_scalar(out=turns[:, r, :, :].rearrange(flat), in0=hang[:].rearrange(flat), scalar1=1.0 / math.pi, scalar2=0.25 - 0.25 * r, op0=ALU.mult, op1=ALU.add)
        for r in range(2):
            nc.vector.scalar_tensor_tensor(out=red[:, r, :, :].rearrange(flat), in0=turns[:, r, :, :].rearrange(flat), scalar=-math.pi, in1=hang[:].rearrange(flat), op0=ALU.mult, op1=ALU.add)
            nc.scalar.activation(out=sn[:, r, :, :].rearrange(flat), in_=red[:, r, :, :].rearrange(flat), func=ACT.Sin, bias=-0.25 * math.pi * r)
        for r in range(2):
            nc.vector.tensor_tensor(out=sq[:, r, :, :].rearrange(flat), in0=sn[:, r, :, :].rearrange(flat), in1=sn[:, r, :, :].rearrange(flat), op=ALU.mult)
        tab = keep.tile([P, TT, 2, HD], F32, name="tab", align_bytes=256)
        nc.vector.tensor_scalar(
            out=tab[:, :, 0, :].rearrange("p a (h j) -> p a h j", h=2),
            in0=sq[:, 0, :, :].unsqueeze(2).to_broadcast([P, TT, 2, HALF]),
            scalar1=-2.0, scalar2=1.0, op0=ALU.mult, op1=ALU.add,
        )
        nc.vector.tensor_scalar(out=tab[:, :, 1, 0:HALF], in0=sq[:, 1, :, :], scalar1=-2.0, scalar2=1.0, op0=ALU.mult, op1=ALU.add)
        nc.vector.tensor_scalar(out=tab[:, :, 1, HALF:HD], in0=sq[:, 1, :, :], scalar1=2.0, scalar2=-1.0, op0=ALU.mult, op1=ALU.add)

        def project(codes, cblk, planes, pblk, a):
            acc = psum.tile([P, 512], F32, name="acc")
            for g in range(PASSES):
                nc.tensor.matmul_mx(
                    out=acc[:],
                    lhsT=xc[:, g, 256 * a : 256 * (a + 1)].bitcast(FP4X4),
                    lhsT_scale=xs[:, g, P * a : P * (a + 1)],
                    rhs=codes[:, g, 1024 * cblk : 1024 * (cblk + 1)].bitcast(FP4X4),
                    rhs_scale=planes[:, g, 512 * pblk : 512 * (pblk + 1)],
                    start=(g == 0),
                    stop=(g == PASSES - 1),
                )
            return acc

        def mult(acc_view, heads, a, dst):
            nc.vector.tensor_tensor(
                out=dst.rearrange("p r (h d) -> p r h d", h=heads),
                in0=acc_view.unsqueeze(1).to_broadcast([P, 2, heads, HD]),
                in1=tab[:, a, :, :].unsqueeze(2).to_broadcast([P, 2, heads, HD]),
                op=ALU.mult,
            )

        def q_bank(t, a, ut, col):
            if t < 2:
                acc = project(qc0 if t == 0 else qc1, 0, qs01, t, a)
            else:
                acc = project(qc23, t - 2, qc0, t - 2, a)
            mult(acc[:].rearrange("p (h d) -> p h d", h=4), 4, a, ut[:, :, col : col + 512])

        def kv_bank(t, a, blk, ut, col, ov, vector_first):
            if t == 0:
                acc = project(kvc0, blk, kvs0, blk, a)
            elif t == 1:
                acc = project(kvc1, blk, qc1, blk, a)
            else:
                acc = project(kvcr, 2 * (t - 2) + blk, kvc0, 2 * (t - 2) + blk, a)
            view = acc[:].rearrange("p (h w d) -> p h w d", h=2, w=2)
            if vector_first:
                mult(view[:, :, 0, :], 2, a, ut[:, :, col : col + 256])
            nc.scalar.copy(out=ov[:, 256 * blk : 256 * (blk + 1)].rearrange("p (h d) -> p h d", h=2), in_=view[:, :, 1, :])
            if not vector_first:
                mult(view[:, :, 0, :], 2, a, ut[:, :, col : col + 256])

        def store(dst, head, heads, a, src):
            nc.sync.dma_start(out=dst[0, P * a : P * (a + 1), head : head + heads, :].rearrange("s h d -> s (h d)"), in_=src)

        def rope_add(eng, ut, o, cols=slice(None)):
            split = "p (h w j) -> p h w j"
            eng.tensor_tensor(
                out=o[:, cols].rearrange(split, w=2, j=HALF),
                in0=ut[:, 0, cols].rearrange(split, w=2, j=HALF),
                in1=ut[:, 1, cols].rearrange(split, w=2, j=HALF)[:, :, ::-1, :],
                op=ALU.add,
            )

        held = []

        def step(fresh, hold=2):
            held.append(fresh)
            for k in range(len(held) - hold):
                for args in held[0]:
                    store(*args)
                held.remove(held[0])

        def first_unit():
            ut = work.tile([P, 2, 512], F32, name="ut")
            o = work.tile([P, 512], F32, name="o", align_bytes=256)
            split = "p (h w j) -> p h w j"
            for half in range(2):
                acc = psum.tile([P, 512], F32, name="acc")
                for g in range(PASSES):
                    nc.tensor.matmul_mx(
                        out=acc[:, 0:256],
                        lhsT=xc[:, g, 0:256].bitcast(FP4X4),
                        lhsT_scale=xs[:, g, 0:P],
                        rhs=qc0[:, g, 512 * half : 512 * (half + 1)].bitcast(FP4X4),
                        rhs_scale=qs01[:, g, 256 * half : 256 * (half + 1)],
                        start=(g == 0),
                        stop=(g == PASSES - 1),
                    )
                cols = slice(256 * half, 256 * (half + 1))
                mult(acc[:, 0:256].rearrange("p (h d) -> p h d", h=2), 2, 0, ut[:, :, cols])
                nc.gpsimd.tensor_tensor(
                    out=o[:, cols].rearrange(split, w=2, j=HALF),
                    in0=ut[:, 0, cols].rearrange(split, w=2, j=HALF),
                    in1=ut[:, 1, cols].rearrange(split, w=2, j=HALF)[:, :, ::-1, :],
                    op=ALU.add,
                )
            step([(out_q, 0, 4, 0, o[:])])

        def q_phase(t, span, freed=None, first=0):
            for a0 in range(first, TT, span):
                ut = work.tile([P, 2, 512 * span], F32, name="ut")
                for i in range(span):
                    q_bank(t, a0 + i, ut, 512 * i)
                if freed is not None and a0 + span == TT:
                    freed()
                o = work.tile([P, 512 * span], F32, name="o", align_bytes=256)
                rope_add(nc.gpsimd, ut, o)
                step([(out_q, 4 * t, 4, a0 + i, o[:, 512 * i : 512 * (i + 1)]) for i in range(span)])

        def kv_phase(t, span, freed=None):
            for a0 in range(0, TT, span):
                ut = work.tile([P, 2, 512 * span], F32, name="ut")
                for i in range(span):
                    ov = work.tile([P, 512], F32, name="ov", align_bytes=256)
                    kv_bank(t, a0 + i, 0, ut, 512 * i, ov, True)
                    kv_bank(t, a0 + i, 1, ut, 512 * i + 256, ov, True)
                    if freed is not None and a0 + i + 1 == TT:
                        freed()
                    store(out_v, 4 * t, 4, a0 + i, ov[:])
                    if i + 1 < span:
                        step([])
                o = work.tile([P, 512 * span], F32, name="o", align_bytes=256)
                rope_add(nc.gpsimd, ut, o)
                step([(out_k, 4 * t, 4, a0 + i, o[:, 512 * i : 512 * (i + 1)]) for i in range(span)])

        def last_kv_phase(t):
            for a in range(TT - 1):
                ut = work.tile([P, 2, 512], F32, name="ut")
                ov = work.tile([P, 512], F32, name="ov", align_bytes=256)
                kv_bank(t, a, 0, ut, 0, ov, True)
                kv_bank(t, a, 1, ut, 256, ov, True)
                store(out_v, 4 * t, 4, a, ov[:])
                o = work.tile([P, 512], F32, name="o", align_bytes=256)
                rope_add(nc.gpsimd, ut, o)
                step([(out_k, 4 * t, 4, a, o[:])], 1)
            a = TT - 1
            ut = work.tile([P, 2, 512], F32, name="ut")
            ov = work.tile([P, 512], F32, name="ov", align_bytes=256)
            o = work.tile([P, 512], F32, name="o", align_bytes=256)
            for w in range(2):
                for pair in range(2):
                    blk = 2 * (t - 2) + pair
                    acc = psum.tile([P, 512], F32, name="acc")
                    for h in range(2):
                        for g in range(PASSES):
                            nc.tensor.matmul_mx(
                                out=acc[:, HD * h : HD * (h + 1)],
                                lhsT=xc[:, g, 256 * a : 256 * (a + 1)].bitcast(FP4X4),
                                lhsT_scale=xs[:, g, P * a : P * (a + 1)],
                                rhs=kvcr[:, g, 1024 * blk + 512 * h + 256 * w : 1024 * blk + 512 * h + 256 * (w + 1)].bitcast(FP4X4),
                                rhs_scale=kvc0[:, g, 512 * blk + 256 * h + HD * w : 512 * blk + 256 * h + HD * (w + 1)],
                                start=(g == 0),
                                stop=(g == PASSES - 1),
                            )
                    cols = slice(256 * pair, 256 * (pair + 1))
                    if w == 0:
                        mult(acc[:, 0:256].rearrange("p (h d) -> p h d", h=2), 2, a, ut[:, :, cols])
                    else:
                        nc.scalar.copy(out=ov[:, cols], in_=acc[:, 0:256])
            rope_add(nc.vector, ut, o)
            store(out_v, 4 * t, 4, a, ov[:])
            step([], 0)
            store(out_k, 4 * t, 4, a, o[:])

        def after_q1():
            load_scales(qc1, wkv_scales, 1024, 2048)
            load_codes(kvcr, wkv_words, 4096, 8192)

        first_unit()
        q_phase(0, 1, lambda: load_scales(qc0, wq_scales, 1024, 2048), 1)
        q_phase(1, 2, after_q1)
        kv_phase(0, 2, lambda: load_scales(kvc0, wkv_scales, 2048, 4096))
        q_phase(2, 2)
        q_phase(3, 2)
        kv_phase(1, 2)
        kv_phase(2, 2)
        last_kv_phase(3)
